import numpy as np
import ml_dtypes

BF16 = ml_dtypes.bfloat16


def bf(x):
    return np.asarray(x, np.float32).astype(BF16)


def f32(x):
    return np.asarray(x, np.float32)


def f64(x):
    return np.asarray(x).astype(np.float64)


def striped(idx):
    return np.tile(idx.reshape(-1, 16).T, (8, 1))


S, D, M, N = 1024, 128, 256, 128
EPS = 1e-5


def setup_inputs():
    return {'tok_emb': bf(np.random.standard_normal((D, S))), 'emb_norm_w': f32(1.0 + 0.1 * np.random.standard_normal((D, 1))), 'w': bf(np.random.standard_normal((D, M)) / np.sqrt(D)), 'offs': striped(np.random.permutation(np.tile(np.arange(S), 2))[:N])}


def reference(tok_emb, emb_norm_w, w, offs):
    idx = offs[:16].T.reshape(-1)
    t = f64(tok_emb)
    mu = t.mean(axis=0, keepdims=True)
    var = ((t - mu) ** 2).mean(axis=0, keepdims=True)
    xn = (t - mu) / np.sqrt(var + EPS) * f64(emb_norm_w)
    return f64(w).T @ xn[:, idx]

@@ -1,0 +1,74 @@
+import concourse.mybir as mybir
+
+BF16, F32, U16 = mybir.dt.bfloat16, mybir.dt.float32, mybir.dt.uint16
+FUNC = mybir.ActivationFunctionType
+ALU = mybir.AluOpType
+
+D, S, M, N = 128, 1024, 256, 128
+EPS = 1e-5
+HALF = 512
+FLOPS = 2 * D * M * N
+
+
+def tile_bertrewardmodel_kernel(tc, tok_emb, emb_norm_w, w, offs, out):
+    nc = tc.nc
+    with (
+        tc.tile_pool(name="held", bufs=1) as held,
+        tc.psum_pool(name="psum", bufs=1) as psum,
+    ):
+        raw = [held.tile([D, HALF], BF16, name=f"raw{h}") for h in range(2)]
+        nc.sync.dma_start(raw[0][:], tok_emb[:, 0:HALF])
+        nc.scalar.dma_start(raw[1][:], tok_emb[:, HALF:S])
+        offsets = held.tile([D, N // 16], U16, name="offsets")
+        nc.sync.dma_start(offsets[:], offs)
+        gain = held.tile([D, 1], F32, name="gain")
+        nc.scalar.dma_start(gain[:], emb_norm_w)
+        weights = held.tile([D, M], BF16, name="weights")
+        nc.sync.dma_start(weights[:], w)
+
+        centring = held.tile([D, D], BF16, name="centring")
+        nc.gpsimd.memset(centring[:], -1.0 / D)
+        nc.gpsimd.affine_select(
+            out=centring[:],
+            in_=centring[:],
+            compare_op=ALU.not_equal,
+            fill=1.0 - 1.0 / D,
+            base=0,
+            pattern=[[-1, D]],
+            channel_multiplier=1,
+        )
+        averaging = held.tile([D, D], F32, name="averaging")
+        nc.vector.memset(averaging[:], 1.0 / D)
+        eps = held.tile([D, 1], F32, name="eps")
+        nc.vector.memset(eps[:], EPS)
+
+        xn = held.tile([D, S], BF16, name="xn")
+        for h in range(2):
+            centred = psum.tile([D, HALF], F32, name=f"centred{h}")
+            nc.tensor.matmul(centred[:], centring[:], raw[h][:], start=True, stop=True)
+            squares = held.tile([D, HALF], F32, name=f"squares{h}")
+            nc.scalar.activation(squares[:], centred[:], FUNC.Square)
+            variance = psum.tile([D, HALF], F32, name=f"variance{h}")
+            nc.tensor.matmul(variance[:], averaging[:], squares[:], start=True, stop=True)
+            rstd = held.tile([D, HALF], F32, name=f"rstd{h}")
+            nc.scalar.activation(rstd[:], variance[:], FUNC.Abs_reciprocal_sqrt, bias=eps[:])
+            nc.vector.scalar_tensor_tensor(
+                xn[:, h * HALF : (h + 1) * HALF],
+                centred[:],
+                gain[:],
+                rstd[:],
+                ALU.mult,
+                ALU.mult,
+            )
+
+        queries = psum.tile([D, N], F32, name="queries")
+        nc.tensor.matmul(queries[:], weights[:, 0:D], xn[:].indirect(offsets[:]), start=True, stop=True)
+        keys = psum.tile([D, N], F32, name="keys")
+        nc.tensor.matmul(keys[:], weights[:, D:M], xn[:].indirect(offsets[:]), start=True, stop=True)
+
+        queries_out = held.tile([D, N], F32, name="queries_out")
+        nc.vector.tensor_copy(queries_out[:], queries[:])
+        nc.sync.dma_start(out[0:D, :], queries_out[:])
+        keys_out = held.tile([D, N], F32, name="keys_out")
+        nc.scalar.copy(keys_out[:], keys[:])
+        nc.scalar.dma_start(out[D:M, :], keys_out[:])

@@ -7,6 +7,7 @@ ALU = mybir.AluOpType
 D, S, M, N = 128, 1024, 256, 128
 EPS = 1e-5
 HALF = 512
+WARM_UPS = 4
 FLOPS = 2 * D * M * N
 
 
@@ -26,6 +27,17 @@ def tile_bertrewardmodel_kernel(tc, tok_emb, emb_norm_w, w, offs, out):
         weights = held.tile([D, M], BF16, name="weights")
         nc.sync.dma_start(weights[:], w)
 
+        zeros = held.tile([D, HALF], BF16, name="zeros")
+        nc.vector.memset(zeros[:], 0.0)
+        unread = psum.tile([D, HALF], F32, name="unread")
+        for repeat in range(WARM_UPS):
+            nc.tensor.matmul(unread[:], zeros[:, 0:D], zeros[:], start=True, stop=True)
+
+        eps = held.tile([D, 1], F32, name="eps")
+        nc.vector.memset(eps[:], EPS)
+        unused = held.tile([D, 1], F32, name="unused")
+        nc.scalar.activation(unused[:], eps[:], FUNC.Abs_reciprocal_sqrt)
+
         centring = held.tile([D, D], BF16, name="centring")
         nc.gpsimd.memset(centring[:], -1.0 / D)
         nc.gpsimd.affine_select(
@@ -39,8 +51,6 @@ def tile_bertrewardmodel_kernel(tc, tok_emb, emb_norm_w, w, offs, out):
         )
         averaging = held.tile([D, D], F32, name="averaging")
         nc.vector.memset(averaging[:], 1.0 / D)
-        eps = held.tile([D, 1], F32, name="eps")
-        nc.vector.memset(eps[:], EPS)
 
         xn = held.tile([D, S], BF16, name="xn")
         for h in range(2):

@@ -6,8 +6,9 @@ ALU = mybir.AluOpType
 
 D, S, M, N = 128, 1024, 256, 128
 EPS = 1e-5
-HALF = 512
-WARM_UPS = 4
+PIECES = 4
+P = S // PIECES
+WARM_UPS = 10
 FLOPS = 2 * D * M * N
 
 
@@ -16,22 +17,23 @@ def tile_bertrewardmodel_kernel(tc, tok_emb, emb_norm_w, w, offs, out):
     with (
         tc.tile_pool(name="held", bufs=1) as held,
         tc.psum_pool(name="psum", bufs=1) as psum,
+        tc.psum_pool(name="turning", bufs=2) as turning,
     ):
-        raw = [held.tile([D, HALF], BF16, name=f"raw{h}") for h in range(2)]
-        nc.sync.dma_start(raw[0][:], tok_emb[:, 0:HALF])
-        nc.scalar.dma_start(raw[1][:], tok_emb[:, HALF:S])
+        zeros = held.tile([D, D], BF16, name="zeros")
+        nc.gpsimd.memset(zeros[:], 0.0)
+        queries = psum.tile([D, N], F32, name="queries")
+        for repeat in range(WARM_UPS):
+            nc.tensor.matmul(queries[:], zeros[:], zeros[:], start=True, stop=True)
+
+        raw = [held.tile([D, P], BF16, name=f"raw{c}") for c in range(PIECES)]
+        for c in range(PIECES):
+            nc.sync.dma_start(raw[c][:], tok_emb[:, c * P : (c + 1) * P])
+        gain = held.tile([D, 1], F32, name="gain")
+        nc.sync.dma_start(gain[:], emb_norm_w)
         offsets = held.tile([D, N // 16], U16, name="offsets")
         nc.sync.dma_start(offsets[:], offs)
-        gain = held.tile([D, 1], F32, name="gain")
-        nc.scalar.dma_start(gain[:], emb_norm_w)
         weights = held.tile([D, M], BF16, name="weights")
         nc.sync.dma_start(weights[:], w)
-
-        zeros = held.tile([D, HALF], BF16, name="zeros")
-        nc.vector.memset(zeros[:], 0.0)
-        unread = psum.tile([D, HALF], F32, name="unread")
-        for repeat in range(WARM_UPS):
-            nc.tensor.matmul(unread[:], zeros[:, 0:D], zeros[:], start=True, stop=True)
 
         eps = held.tile([D, 1], F32, name="eps")
         nc.vector.memset(eps[:], EPS)
@@ -52,26 +54,23 @@ def tile_bertrewardmodel_kernel(tc, tok_emb, emb_norm_w, w, offs, out):
         averaging = held.tile([D, D], F32, name="averaging")
         nc.vector.memset(averaging[:], 1.0 / D)
 
+        centred = [psum.tile([D, P], F32, name=f"centred{c}") for c in range(PIECES)]
+        for c in range(PIECES):
+            nc.tensor.matmul(centred[c][:], centring[:], raw[c][:], start=True, stop=True)
+        squares = [held.tile([D, P], F32, name=f"squares{c}") for c in range(PIECES)]
+        for c in range(PIECES):
+            nc.scalar.activation(squares[c][:], centred[c][:], FUNC.Square)
+
         xn = held.tile([D, S], BF16, name="xn")
-        for h in range(2):
-            centred = psum.tile([D, HALF], F32, name=f"centred{h}")
-            nc.tensor.matmul(centred[:], centring[:], raw[h][:], start=True, stop=True)
-            squares = held.tile([D, HALF], F32, name=f"squares{h}")
-            nc.scalar.activation(squares[:], centred[:], FUNC.Square)
-            variance = psum.tile([D, HALF], F32, name=f"variance{h}")
-            nc.tensor.matmul(variance[:], averaging[:], squares[:], start=True, stop=True)
-            rstd = held.tile([D, HALF], F32, name=f"rstd{h}")
+        for c in range(PIECES):
+            variance = turning.tile([D, P], F32, name="variance")
+            nc.tensor.matmul(variance[:], averaging[:], squares[c][:], start=True, stop=True)
+            rstd = held.tile([D, P], F32, name=f"rstd{c}")
             nc.scalar.activation(rstd[:], variance[:], FUNC.Abs_reciprocal_sqrt, bias=eps[:])
             nc.vector.scalar_tensor_tensor(
-                xn[:, h * HALF : (h + 1) * HALF],
-                centred[:],
-                gain[:],
-                rstd[:],
-                ALU.mult,
-                ALU.mult,
+                xn[:, c * P : (c + 1) * P], centred[c][:], gain[:], rstd[:], ALU.mult, ALU.mult
             )
 
-        queries = psum.tile([D, N], F32, name="queries")
         nc.tensor.matmul(queries[:], weights[:, 0:D], xn[:].indirect(offsets[:]), start=True, stop=True)
         keys = psum.tile([D, N], F32, name="keys")
         nc.tensor.matmul(keys[:], weights[:, D:M], xn[:].indirect(offsets[:]), start=True, stop=True)

@@ -6,8 +6,10 @@ ALU = mybir.AluOpType
 
 D, S, M, N = 128, 1024, 256, 128
 EPS = 1e-5
-PIECES = 4
-P = S // PIECES
+WIDTHS = (128, 256, 256, 256, 128)
+STARTS = tuple(sum(WIDTHS[:c]) for c in range(len(WIDTHS)))
+assert sum(WIDTHS) == S
+PIECES = len(WIDTHS)
 WARM_UPS = 10
 FLOPS = 2 * D * M * N
 
@@ -17,17 +19,18 @@ def tile_bertrewardmodel_kernel(tc, tok_emb, emb_norm_w, w, offs, out):
     with (
         tc.tile_pool(name="held", bufs=1) as held,
         tc.psum_pool(name="psum", bufs=1) as psum,
-        tc.psum_pool(name="turning", bufs=2) as turning,
+        tc.psum_pool(name="turning", bufs=3) as turning,
     ):
+
         zeros = held.tile([D, D], BF16, name="zeros")
         nc.gpsimd.memset(zeros[:], 0.0)
-        queries = psum.tile([D, N], F32, name="queries")
+        unread = turning.tile([D, D], F32, name="unread", tag="bank")
         for repeat in range(WARM_UPS):
-            nc.tensor.matmul(queries[:], zeros[:], zeros[:], start=True, stop=True)
+            nc.tensor.matmul(unread[:], zeros[:], zeros[:], start=True, stop=True)
 
-        raw = [held.tile([D, P], BF16, name=f"raw{c}") for c in range(PIECES)]
+        raw = [held.tile([D, WIDTHS[c]], BF16, name=f"raw{c}") for c in range(PIECES)]
         for c in range(PIECES):
-            nc.sync.dma_start(raw[c][:], tok_emb[:, c * P : (c + 1) * P])
+            nc.sync.dma_start(raw[c][:], tok_emb[:, STARTS[c] : STARTS[c] + WIDTHS[c]])
         gain = held.tile([D, 1], F32, name="gain")
         nc.sync.dma_start(gain[:], emb_norm_w)
         offsets = held.tile([D, N // 16], U16, name="offsets")
@@ -54,25 +57,26 @@ def tile_bertrewardmodel_kernel(tc, tok_emb, emb_norm_w, w, offs, out):
         averaging = held.tile([D, D], F32, name="averaging")
         nc.vector.memset(averaging[:], 1.0 / D)
 
-        centred = [psum.tile([D, P], F32, name=f"centred{c}") for c in range(PIECES)]
+        centred = [psum.tile([D, WIDTHS[c]], F32, name=f"centred{c}") for c in range(PIECES)]
         for c in range(PIECES):
             nc.tensor.matmul(centred[c][:], centring[:], raw[c][:], start=True, stop=True)
-        squares = [held.tile([D, P], F32, name=f"squares{c}") for c in range(PIECES)]
+        squares = [held.tile([D, WIDTHS[c]], F32, name=f"squares{c}") for c in range(PIECES)]
         for c in range(PIECES):
             nc.scalar.activation(squares[c][:], centred[c][:], FUNC.Square)
 
         xn = held.tile([D, S], BF16, name="xn")
         for c in range(PIECES):
-            variance = turning.tile([D, P], F32, name="variance")
+            variance = turning.tile([D, WIDTHS[c]], F32, name="variance", tag="bank")
             nc.tensor.matmul(variance[:], averaging[:], squares[c][:], start=True, stop=True)
-            rstd = held.tile([D, P], F32, name=f"rstd{c}")
+            rstd = held.tile([D, WIDTHS[c]], F32, name=f"rstd{c}")
             nc.scalar.activation(rstd[:], variance[:], FUNC.Abs_reciprocal_sqrt, bias=eps[:])
             nc.vector.scalar_tensor_tensor(
-                xn[:, c * P : (c + 1) * P], centred[c][:], gain[:], rstd[:], ALU.mult, ALU.mult
+                xn[:, STARTS[c] : STARTS[c] + WIDTHS[c]], centred[c][:], gain[:], rstd[:], ALU.mult, ALU.mult
             )
 
+        queries = turning.tile([D, N], F32, name="queries", tag="bank")
         nc.tensor.matmul(queries[:], weights[:, 0:D], xn[:].indirect(offsets[:]), start=True, stop=True)
-        keys = psum.tile([D, N], F32, name="keys")
+        keys = turning.tile([D, N], F32, name="keys", tag="bank")
         nc.tensor.matmul(keys[:], weights[:, D:M], xn[:].indirect(offsets[:]), start=True, stop=True)
 
         queries_out = held.tile([D, N], F32, name="queries_out")

@@ -10,7 +10,6 @@ WIDTHS = (128, 256, 256, 256, 128)
 STARTS = tuple(sum(WIDTHS[:c]) for c in range(len(WIDTHS)))
 assert sum(WIDTHS) == S
 PIECES = len(WIDTHS)
-WARM_UPS = 10
 FLOPS = 2 * D * M * N
 
 
@@ -21,12 +20,6 @@ def tile_bertrewardmodel_kernel(tc, tok_emb, emb_norm_w, w, offs, out):
         tc.psum_pool(name="psum", bufs=1) as psum,
         tc.psum_pool(name="turning", bufs=3) as turning,
     ):
-
-        zeros = held.tile([D, D], BF16, name="zeros")
-        nc.gpsimd.memset(zeros[:], 0.0)
-        unread = turning.tile([D, D], F32, name="unread", tag="bank")
-        for repeat in range(WARM_UPS):
-            nc.tensor.matmul(unread[:], zeros[:], zeros[:], start=True, stop=True)
 
         raw = [held.tile([D, WIDTHS[c]], BF16, name=f"raw{c}") for c in range(PIECES)]
         for c in range(PIECES):

@@ -6,10 +6,11 @@ ALU = mybir.AluOpType
 
 D, S, M, N = 128, 1024, 256, 128
 EPS = 1e-5
-WIDTHS = (128, 256, 256, 256, 128)
+WIDTHS = (128, 384, 384, 128)
 STARTS = tuple(sum(WIDTHS[:c]) for c in range(len(WIDTHS)))
 assert sum(WIDTHS) == S
 PIECES = len(WIDTHS)
+WARM_UPS = 10
 FLOPS = 2 * D * M * N
 
 
@@ -20,6 +21,12 @@ def tile_bertrewardmodel_kernel(tc, tok_emb, emb_norm_w, w, offs, out):
         tc.psum_pool(name="psum", bufs=1) as psum,
         tc.psum_pool(name="turning", bufs=3) as turning,
     ):
+
+        zeros = held.tile([D, D], BF16, name="zeros")
+        nc.gpsimd.memset(zeros[:], 0.0)
+        unread = turning.tile([D, D], F32, name="unread", tag="bank")
+        for repeat in range(WARM_UPS):
+            nc.tensor.matmul(unread[:], zeros[:], zeros[:], start=True, stop=True)
 
         raw = [held.tile([D, WIDTHS[c]], BF16, name=f"raw{c}") for c in range(PIECES)]
         for c in range(PIECES):

@@ -10,6 +10,8 @@ WIDTHS = (128, 384, 384, 128)
 STARTS = tuple(sum(WIDTHS[:c]) for c in range(len(WIDTHS)))
 assert sum(WIDTHS) == S
 PIECES = len(WIDTHS)
+RUN = 128
+assert all(width % RUN == 0 for width in WIDTHS)
 WARM_UPS = 10
 FLOPS = 2 * D * M * N
 
@@ -69,10 +71,16 @@ def tile_bertrewardmodel_kernel(tc, tok_emb, emb_norm_w, w, offs, out):
             variance = turning.tile([D, WIDTHS[c]], F32, name="variance", tag="bank")
             nc.tensor.matmul(variance[:], averaging[:], squares[c][:], start=True, stop=True)
             rstd = held.tile([D, WIDTHS[c]], F32, name=f"rstd{c}")
-            nc.scalar.activation(rstd[:], variance[:], FUNC.Abs_reciprocal_sqrt, bias=eps[:])
-            nc.vector.scalar_tensor_tensor(
-                xn[:, STARTS[c] : STARTS[c] + WIDTHS[c]], centred[c][:], gain[:], rstd[:], ALU.mult, ALU.mult
-            )
+            for lo in range(0, WIDTHS[c], RUN):
+                nc.scalar.activation(rstd[:, lo : lo + RUN], variance[:, lo : lo + RUN], FUNC.Abs_reciprocal_sqrt, bias=eps[:])
+                nc.vector.scalar_tensor_tensor(
+                    xn[:, STARTS[c] + lo : STARTS[c] + lo + RUN],
+                    centred[c][:, lo : lo + RUN],
+                    gain[:],
+                    rstd[:, lo : lo + RUN],
+                    ALU.mult,
+                    ALU.mult,
+                )
 
         queries = turning.tile([D, N], F32, name="queries", tag="bank")
         nc.tensor.matmul(queries[:], weights[:, 0:D], xn[:].indirect(offsets[:]), start=True, stop=True)

@@ -88,8 +88,8 @@ def tile_bertrewardmodel_kernel(tc, tok_emb, emb_norm_w, w, offs, out):
         nc.tensor.matmul(keys[:], weights[:, D:M], xn[:].indirect(offsets[:]), start=True, stop=True)
 
         queries_out = held.tile([D, N], F32, name="queries_out")
-        nc.vector.tensor_copy(queries_out[:], queries[:])
-        nc.sync.dma_start(out[0:D, :], queries_out[:])
+        nc.scalar.copy(queries_out[:], queries[:])
+        nc.scalar.dma_start(out[0:D, :], queries_out[:])
         keys_out = held.tile([D, N], F32, name="keys_out")
         nc.scalar.copy(keys_out[:], keys[:])
         nc.scalar.dma_start(out[D:M, :], keys_out[:])

@@ -1,4 +1,5 @@
 import concourse.mybir as mybir
+from concourse.masks import make_identity
 
 BF16, F32, U16 = mybir.dt.bfloat16, mybir.dt.float32, mybir.dt.uint16
 FUNC = mybir.ActivationFunctionType
@@ -6,12 +7,9 @@ ALU = mybir.AluOpType
 
 D, S, M, N = 128, 1024, 256, 128
 EPS = 1e-5
-WIDTHS = (128, 384, 384, 128)
-STARTS = tuple(sum(WIDTHS[:c]) for c in range(len(WIDTHS)))
-assert sum(WIDTHS) == S
-PIECES = len(WIDTHS)
-RUN = 128
-assert all(width % RUN == 0 for width in WIDTHS)
+CHUNK = 256
+CHUNKS = S // CHUNK
+BLOCKS = CHUNK // D
 WARM_UPS = 10
 FLOPS = 2 * D * M * N
 
@@ -21,7 +19,7 @@ def tile_bertrewardmodel_kernel(tc, tok_emb, emb_norm_w, w, offs, out):
     with (
         tc.tile_pool(name="held", bufs=1) as held,
         tc.psum_pool(name="psum", bufs=1) as psum,
-        tc.psum_pool(name="turning", bufs=3) as turning,
+        tc.psum_pool(name="turning", bufs=4) as turning,
     ):
 
         zeros = held.tile([D, D], BF16, name="zeros")
@@ -30,9 +28,9 @@ def tile_bertrewardmodel_kernel(tc, tok_emb, emb_norm_w, w, offs, out):
         for repeat in range(WARM_UPS):
             nc.tensor.matmul(unread[:], zeros[:], zeros[:], start=True, stop=True)
 
-        raw = [held.tile([D, WIDTHS[c]], BF16, name=f"raw{c}") for c in range(PIECES)]
-        for c in range(PIECES):
-            nc.sync.dma_start(raw[c][:], tok_emb[:, STARTS[c] : STARTS[c] + WIDTHS[c]])
+        raw = [held.tile([D, CHUNK], BF16, name=f"raw{c}") for c in range(CHUNKS)]
+        for c in range(CHUNKS):
+            nc.sync.dma_start(raw[c][:], tok_emb[:, c * CHUNK : (c + 1) * CHUNK])
         gain = held.tile([D, 1], F32, name="gain")
         nc.sync.dma_start(gain[:], emb_norm_w)
         offsets = held.tile([D, N // 16], U16, name="offsets")
@@ -56,31 +54,49 @@ def tile_bertrewardmodel_kernel(tc, tok_emb, emb_norm_w, w, offs, out):
             pattern=[[-1, D]],
             channel_multiplier=1,
         )
-        averaging = held.tile([D, D], F32, name="averaging")
-        nc.vector.memset(averaging[:], 1.0 / D)
+        identity = held.tile([D, D], F32, name="identity")
+        make_identity(nc, identity[:])
 
-        centred = [psum.tile([D, WIDTHS[c]], F32, name=f"centred{c}") for c in range(PIECES)]
-        for c in range(PIECES):
-            nc.tensor.matmul(centred[c][:], centring[:], raw[c][:], start=True, stop=True)
-        squares = [held.tile([D, WIDTHS[c]], F32, name=f"squares{c}") for c in range(PIECES)]
-        for c in range(PIECES):
-            nc.scalar.activation(squares[c][:], centred[c][:], FUNC.Square)
+        centred = [psum.tile([D, CHUNK], F32, name=f"centred{c}") for c in range(CHUNKS)]
+        for c in range(CHUNKS):
+            for b in range(BLOCKS):
+                block = slice(b * D, (b + 1) * D)
+                nc.tensor.matmul(centred[c][:, block], raw[c][:, block], centring[:], start=True, stop=True)
+
+        rstd = [held.tile([D, BLOCKS], F32, name=f"rstd{c}") for c in range(CHUNKS)]
+        for c in range(CHUNKS):
+            if c % 2 == 0:
+                halves = held.tile([D, 6 * BLOCKS], F32, name=f"halves{c}")
+                moments = held.tile([D, 2 * BLOCKS], F32, name=f"moments{c}")
+                for b in range(BLOCKS):
+                    nc.vector.bn_stats(halves[:, 6 * b : 6 * (b + 1)], centred[c][:, b * D : (b + 1) * D])
+                    nc.vector.bn_aggr(moments[:, 2 * b : 2 * (b + 1)], halves[:, 6 * b : 6 * (b + 1)])
+                nc.scalar.activation(rstd[c][:], moments[:, 1::2], FUNC.Abs_reciprocal_sqrt, bias=eps[:])
+            else:
+                variance = held.tile([D, BLOCKS], F32, name=f"variance{c}")
+                for b in range(BLOCKS):
+                    squares = held.tile([D, D], BF16, name=f"squares{c}{b}")
+                    nc.scalar.activation(
+                        squares[:], centred[c][:, b * D : (b + 1) * D], FUNC.Square, scale=D**-0.5, accum_out=variance[:, b : b + 1]
+                    )
+                nc.scalar.activation(rstd[c][:], variance[:], FUNC.Abs_reciprocal_sqrt, bias=eps[:])
 
         xn = held.tile([D, S], BF16, name="xn")
-        for c in range(PIECES):
-            variance = turning.tile([D, WIDTHS[c]], F32, name="variance", tag="bank")
-            nc.tensor.matmul(variance[:], averaging[:], squares[c][:], start=True, stop=True)
-            rstd = held.tile([D, WIDTHS[c]], F32, name=f"rstd{c}")
-            for lo in range(0, WIDTHS[c], RUN):
-                nc.scalar.activation(rstd[:, lo : lo + RUN], variance[:, lo : lo + RUN], FUNC.Abs_reciprocal_sqrt, bias=eps[:])
-                nc.vector.scalar_tensor_tensor(
-                    xn[:, STARTS[c] + lo : STARTS[c] + lo + RUN],
-                    centred[c][:, lo : lo + RUN],
-                    gain[:],
-                    rstd[:, lo : lo + RUN],
-                    ALU.mult,
-                    ALU.mult,
-                )
+        for c in range(CHUNKS):
+            back = turning.tile([D, CHUNK], F32, name="back", tag="bank")
+            for b in range(BLOCKS):
+                block = slice(b * D, (b + 1) * D)
+                scaled = held.tile([D, D], F32, name=f"scaled{c}{b}")
+                if c % 2 == 0:
+                    nc.vector.tensor_scalar_mul(scaled[:], centred[c][:, block], rstd[c][:, b : b + 1])
+                else:
+                    nc.scalar.activation(scaled[:], centred[c][:, block], FUNC.Copy, scale=rstd[c][:, b : b + 1])
+                nc.tensor.transpose(back[:, block], scaled[:], identity[:])
+            words = slice(c * CHUNK, (c + 1) * CHUNK)
+            if c % 2 == 0:
+                nc.vector.tensor_scalar_mul(xn[:, words], back[:], gain[:])
+            else:
+                nc.scalar.activation(xn[:, words], back[:], FUNC.Copy, scale=gain[:])
 
         queries = turning.tile([D, N], F32, name="queries", tag="bank")
         nc.tensor.matmul(queries[:], weights[:, 0:D], xn[:].indirect(offsets[:]), start=True, stop=True)

@@ -7,9 +7,8 @@ ALU = mybir.AluOpType
 
 D, S, M, N = 128, 1024, 256, 128
 EPS = 1e-5
-CHUNK = 256
-CHUNKS = S // CHUNK
-BLOCKS = CHUNK // D
+BLOCKS = S // D
+LOADED = 2
 WARM_UPS = 10
 FLOPS = 2 * D * M * N
 
@@ -18,19 +17,18 @@ def tile_bertrewardmodel_kernel(tc, tok_emb, emb_norm_w, w, offs, out):
     nc = tc.nc
     with (
         tc.tile_pool(name="held", bufs=1) as held,
-        tc.psum_pool(name="psum", bufs=1) as psum,
-        tc.psum_pool(name="turning", bufs=4) as turning,
+        tc.psum_pool(name="banks", bufs=8) as banks,
     ):
 
         zeros = held.tile([D, D], BF16, name="zeros")
         nc.gpsimd.memset(zeros[:], 0.0)
-        unread = turning.tile([D, D], F32, name="unread", tag="bank")
+        unread = banks.tile([D, D], F32, name="unread", tag="bank")
         for repeat in range(WARM_UPS):
             nc.tensor.matmul(unread[:], zeros[:], zeros[:], start=True, stop=True)
 
-        raw = [held.tile([D, CHUNK], BF16, name=f"raw{c}") for c in range(CHUNKS)]
-        for c in range(CHUNKS):
-            nc.sync.dma_start(raw[c][:], tok_emb[:, c * CHUNK : (c + 1) * CHUNK])
+        raw = [held.tile([D, LOADED * D], BF16, name=f"raw{c}") for c in range(BLOCKS // LOADED)]
+        for c in range(BLOCKS // LOADED):
+            nc.sync.dma_start(raw[c][:], tok_emb[:, c * LOADED * D : (c + 1) * LOADED * D])
         gain = held.tile([D, 1], F32, name="gain")
         nc.sync.dma_start(gain[:], emb_norm_w)
         offsets = held.tile([D, N // 16], U16, name="offsets")
@@ -57,50 +55,45 @@ def tile_bertrewardmodel_kernel(tc, tok_emb, emb_norm_w, w, offs, out):
         identity = held.tile([D, D], F32, name="identity")
         make_identity(nc, identity[:])
 
-        centred = [psum.tile([D, CHUNK], F32, name=f"centred{c}") for c in range(CHUNKS)]
-        for c in range(CHUNKS):
-            for b in range(BLOCKS):
-                block = slice(b * D, (b + 1) * D)
-                nc.tensor.matmul(centred[c][:, block], raw[c][:, block], centring[:], start=True, stop=True)
+        centred = []
+        for b in range(BLOCKS):
+            turned = banks.tile([D, D], F32, name=f"centred{b}", tag="bank")
+            words = slice(b % LOADED * D, (b % LOADED + 1) * D)
+            nc.tensor.matmul(turned[:], raw[b // LOADED][:, words], centring[:], start=True, stop=True)
+            centred.append(turned)
 
-        rstd = [held.tile([D, BLOCKS], F32, name=f"rstd{c}") for c in range(CHUNKS)]
-        for c in range(CHUNKS):
-            if c % 2 == 0:
-                halves = held.tile([D, 6 * BLOCKS], F32, name=f"halves{c}")
-                moments = held.tile([D, 2 * BLOCKS], F32, name=f"moments{c}")
-                for b in range(BLOCKS):
-                    nc.vector.bn_stats(halves[:, 6 * b : 6 * (b + 1)], centred[c][:, b * D : (b + 1) * D])
-                    nc.vector.bn_aggr(moments[:, 2 * b : 2 * (b + 1)], halves[:, 6 * b : 6 * (b + 1)])
-                nc.scalar.activation(rstd[c][:], moments[:, 1::2], FUNC.Abs_reciprocal_sqrt, bias=eps[:])
+        rstd = [held.tile([D, 1], F32, name=f"rstd{b}") for b in range(BLOCKS)]
+        for b in range(BLOCKS):
+            if b % 2 == 0:
+                halves = held.tile([D, 6], F32, name=f"halves{b}")
+                moments = held.tile([D, 2], F32, name=f"moments{b}")
+                nc.vector.bn_stats(halves[:], centred[b][:])
+                nc.vector.bn_aggr(moments[:], halves[:])
+                variance = moments[:, 1:2]
             else:
-                variance = held.tile([D, BLOCKS], F32, name=f"variance{c}")
-                for b in range(BLOCKS):
-                    squares = held.tile([D, D], BF16, name=f"squares{c}{b}")
-                    nc.scalar.activation(
-                        squares[:], centred[c][:, b * D : (b + 1) * D], FUNC.Square, scale=D**-0.5, accum_out=variance[:, b : b + 1]
-                    )
-                nc.scalar.activation(rstd[c][:], variance[:], FUNC.Abs_reciprocal_sqrt, bias=eps[:])
+                squares = held.tile([D, D], BF16, name=f"squares{b}")
+                mean_square = held.tile([D, 1], F32, name=f"mean_square{b}")
+                nc.scalar.activation(squares[:], centred[b][:], FUNC.Square, scale=D**-0.5, accum_out=mean_square[:])
+                variance = mean_square[:]
+            nc.scalar.activation(rstd[b][:], variance, FUNC.Abs_reciprocal_sqrt, bias=eps[:])
 
         xn = held.tile([D, S], BF16, name="xn")
-        for c in range(CHUNKS):
-            back = turning.tile([D, CHUNK], F32, name="back", tag="bank")
-            for b in range(BLOCKS):
-                block = slice(b * D, (b + 1) * D)
-                scaled = held.tile([D, D], F32, name=f"scaled{c}{b}")
-                if c % 2 == 0:
-                    nc.vector.tensor_scalar_mul(scaled[:], centred[c][:, block], rstd[c][:, b : b + 1])
-                else:
-                    nc.scalar.activation(scaled[:], centred[c][:, block], FUNC.Copy, scale=rstd[c][:, b : b + 1])
-                nc.tensor.transpose(back[:, block], scaled[:], identity[:])
-            words = slice(c * CHUNK, (c + 1) * CHUNK)
-            if c % 2 == 0:
+        for b in range(BLOCKS):
+            scaled = held.tile([D, D], F32, name=f"scaled{b}")
+            back = banks.tile([D, D], F32, name=f"back{b}", tag="bank")
+            words = slice(b * D, (b + 1) * D)
+            if b % 2 == 0:
+                nc.vector.tensor_scalar_mul(scaled[:], centred[b][:], rstd[b][:])
+                nc.tensor.transpose(back[:], scaled[:], identity[:])
                 nc.vector.tensor_scalar_mul(xn[:, words], back[:], gain[:])
             else:
+                nc.scalar.activation(scaled[:], centred[b][:], FUNC.Copy, scale=rstd[b][:])
+                nc.tensor.transpose(back[:], scaled[:], identity[:])
                 nc.scalar.activation(xn[:, words], back[:], FUNC.Copy, scale=gain[:])
 
-        queries = turning.tile([D, N], F32, name="queries", tag="bank")
+        queries = banks.tile([D, N], F32, name="queries", tag="bank")
         nc.tensor.matmul(queries[:], weights[:, 0:D], xn[:].indirect(offsets[:]), start=True, stop=True)
-        keys = turning.tile([D, N], F32, name="keys", tag="bank")
+        keys = banks.tile([D, N], F32, name="keys", tag="bank")
         nc.tensor.matmul(keys[:], weights[:, D:M], xn[:].indirect(offsets[:]), start=True, stop=True)
 
         queries_out = held.tile([D, N], F32, name="queries_out")

@@ -62,32 +62,27 @@ def tile_bertrewardmodel_kernel(tc, tok_emb, emb_norm_w, w, offs, out):
             nc.tensor.matmul(turned[:], raw[b // LOADED][:, words], centring[:], start=True, stop=True)
             centred.append(turned)
 
-        rstd = [held.tile([D, 1], F32, name=f"rstd{b}") for b in range(BLOCKS)]
+        xn = held.tile([D, S], BF16, name="xn")
         for b in range(BLOCKS):
+            scaled = held.tile([D, D], F32, name=f"scaled{b}")
+            rstd = held.tile([D, 1], F32, name=f"rstd{b}")
+            back = banks.tile([D, D], F32, name=f"back{b}", tag="bank")
+            words = slice(b * D, (b + 1) * D)
             if b % 2 == 0:
                 halves = held.tile([D, 6], F32, name=f"halves{b}")
                 moments = held.tile([D, 2], F32, name=f"moments{b}")
                 nc.vector.bn_stats(halves[:], centred[b][:])
                 nc.vector.bn_aggr(moments[:], halves[:])
-                variance = moments[:, 1:2]
-            else:
-                squares = held.tile([D, D], BF16, name=f"squares{b}")
-                mean_square = held.tile([D, 1], F32, name=f"mean_square{b}")
-                nc.scalar.activation(squares[:], centred[b][:], FUNC.Square, scale=D**-0.5, accum_out=mean_square[:])
-                variance = mean_square[:]
-            nc.scalar.activation(rstd[b][:], variance, FUNC.Abs_reciprocal_sqrt, bias=eps[:])
-
-        xn = held.tile([D, S], BF16, name="xn")
-        for b in range(BLOCKS):
-            scaled = held.tile([D, D], F32, name=f"scaled{b}")
-            back = banks.tile([D, D], F32, name=f"back{b}", tag="bank")
-            words = slice(b * D, (b + 1) * D)
-            if b % 2 == 0:
-                nc.vector.tensor_scalar_mul(scaled[:], centred[b][:], rstd[b][:])
+                nc.scalar.activation(rstd[:], moments[:, 1:2], FUNC.Abs_reciprocal_sqrt, bias=eps[:])
+                nc.vector.tensor_scalar_mul(scaled[:], centred[b][:], rstd[:])
                 nc.tensor.transpose(back[:], scaled[:], identity[:])
                 nc.vector.tensor_scalar_mul(xn[:, words], back[:], gain[:])
             else:
-                nc.scalar.activation(scaled[:], centred[b][:], FUNC.Copy, scale=rstd[b][:])
+                squares = held.tile([D, D], BF16, name=f"squares{b}")
+                variance = held.tile([D, 1], F32, name=f"variance{b}")
+                nc.scalar.activation(squares[:], centred[b][:], FUNC.Square, scale=D**-0.5, accum_out=variance[:])
+                nc.scalar.activation(rstd[:], variance[:], FUNC.Abs_reciprocal_sqrt, bias=eps[:])
+                nc.scalar.activation(scaled[:], centred[b][:], FUNC.Copy, scale=rstd[:])
                 nc.tensor.transpose(back[:], scaled[:], identity[:])
                 nc.scalar.activation(xn[:, words], back[:], FUNC.Copy, scale=gain[:])
 
@@ -96,9 +91,7 @@ def tile_bertrewardmodel_kernel(tc, tok_emb, emb_norm_w, w, offs, out):
         keys = banks.tile([D, N], F32, name="keys", tag="bank")
         nc.tensor.matmul(keys[:], weights[:, D:M], xn[:].indirect(offsets[:]), start=True, stop=True)
 
-        queries_out = held.tile([D, N], F32, name="queries_out")
-        nc.scalar.copy(queries_out[:], queries[:])
-        nc.scalar.dma_start(out[0:D, :], queries_out[:])
-        keys_out = held.tile([D, N], F32, name="keys_out")
-        nc.scalar.copy(keys_out[:], keys[:])
-        nc.scalar.dma_start(out[D:M, :], keys_out[:])
+        products = held.tile([D, M // D, N], F32, name="products")
+        nc.vector.tensor_copy(products[:, 0, :], queries[:])
+        nc.scalar.copy(products[:, 1, :], keys[:])
+        nc.scalar.dma_start(out.rearrange("(half p) n -> p half n", p=D), products[:])

import concourse.mybir as mybir
from concourse.masks import make_identity

BF16, F32, U16 = mybir.dt.bfloat16, mybir.dt.float32, mybir.dt.uint16
FUNC = mybir.ActivationFunctionType
ALU = mybir.AluOpType

D, S, M, N = 128, 1024, 256, 128
EPS = 1e-5
BLOCKS = S // D
LOADED = 2
WARM_UPS = 10
FLOPS = 2 * D * M * N


def tile_bertrewardmodel_kernel(tc, tok_emb, emb_norm_w, w, offs, out):
    nc = tc.nc
    with (
        tc.tile_pool(name="held", bufs=1) as held,
        tc.psum_pool(name="banks", bufs=8) as banks,
    ):

        zeros = held.tile([D, D], BF16, name="zeros")
        nc.gpsimd.memset(zeros[:], 0.0)
        unread = banks.tile([D, D], F32, name="unread", tag="bank")
        for repeat in range(WARM_UPS):
            nc.tensor.matmul(unread[:], zeros[:], zeros[:], start=True, stop=True)

        raw = [held.tile([D, LOADED * D], BF16, name=f"raw{c}") for c in range(BLOCKS // LOADED)]
        for c in range(BLOCKS // LOADED):
            nc.sync.dma_start(raw[c][:], tok_emb[:, c * LOADED * D : (c + 1) * LOADED * D])
        gain = held.tile([D, 1], F32, name="gain")
        nc.sync.dma_start(gain[:], emb_norm_w)
        offsets = held.tile([D, N // 16], U16, name="offsets")
        nc.sync.dma_start(offsets[:], offs)
        weights = held.tile([D, M], BF16, name="weights")
        nc.sync.dma_start(weights[:], w)

        eps = held.tile([D, 1], F32, name="eps")
        nc.vector.memset(eps[:], EPS)
        unused = held.tile([D, 1], F32, name="unused")
        nc.scalar.activation(unused[:], eps[:], FUNC.Abs_reciprocal_sqrt)

        centring = held.tile([D, D], BF16, name="centring")
        nc.gpsimd.memset(centring[:], -1.0 / D)
        nc.gpsimd.affine_select(
            out=centring[:],
            in_=centring[:],
            compare_op=ALU.not_equal,
            fill=1.0 - 1.0 / D,
            base=0,
            pattern=[[-1, D]],
            channel_multiplier=1,
        )
        identity = held.tile([D, D], F32, name="identity")
        make_identity(nc, identity[:])

        centred = []
        for b in range(BLOCKS):
            turned = banks.tile([D, D], F32, name=f"centred{b}", tag="bank")
            words = slice(b % LOADED * D, (b % LOADED + 1) * D)
            nc.tensor.matmul(turned[:], raw[b // LOADED][:, words], centring[:], start=True, stop=True)
            centred.append(turned)

        xn = held.tile([D, S], BF16, name="xn")
        for b in range(BLOCKS):
            scaled = held.tile([D, D], F32, name=f"scaled{b}")
            rstd = held.tile([D, 1], F32, name=f"rstd{b}")
            back = banks.tile([D, D], F32, name=f"back{b}", tag="bank")
            words = slice(b * D, (b + 1) * D)
            if b % 2 == 0:
                halves = held.tile([D, 6], F32, name=f"halves{b}")
                moments = held.tile([D, 2], F32, name=f"moments{b}")
                nc.vector.bn_stats(halves[:], centred[b][:])
                nc.vector.bn_aggr(moments[:], halves[:])
                nc.scalar.activation(rstd[:], moments[:, 1:2], FUNC.Abs_reciprocal_sqrt, bias=eps[:])
                nc.vector.tensor_scalar_mul(scaled[:], centred[b][:], rstd[:])
                nc.tensor.transpose(back[:], scaled[:], identity[:])
                nc.vector.tensor_scalar_mul(xn[:, words], back[:], gain[:])
            else:
                squares = held.tile([D, D], BF16, name=f"squares{b}")
                variance = held.tile([D, 1], F32, name=f"variance{b}")
                nc.scalar.activation(squares[:], centred[b][:], FUNC.Square, scale=D**-0.5, accum_out=variance[:])
                nc.scalar.activation(rstd[:], variance[:], FUNC.Abs_reciprocal_sqrt, bias=eps[:])
                nc.scalar.activation(scaled[:], centred[b][:], FUNC.Copy, scale=rstd[:])
                nc.tensor.transpose(back[:], scaled[:], identity[:])
                nc.scalar.activation(xn[:, words], back[:], FUNC.Copy, scale=gain[:])

        queries = banks.tile([D, N], F32, name="queries", tag="bank")
        nc.tensor.matmul(queries[:], weights[:, 0:D], xn[:].indirect(offsets[:]), start=True, stop=True)
        keys = banks.tile([D, N], F32, name="keys", tag="bank")
        nc.tensor.matmul(keys[:], weights[:, D:M], xn[:].indirect(offsets[:]), start=True, stop=True)

        products = held.tile([D, M // D, N], F32, name="products")
        nc.vector.tensor_copy(products[:, 0, :], queries[:])
        nc.scalar.copy(products[:, 1, :], keys[:])
        nc.scalar.dma_start(out.rearrange("(half p) n -> p half n", p=D), products[:])
